import numpy as np
import ml_dtypes


def mxq(x, axis, fmt="e4m3"):
    dtype, down = {"e4m3": (ml_dtypes.float8_e4m3fn, 7), "e5m2": (ml_dtypes.float8_e5m2, 14)}[fmt]
    v = np.moveaxis(np.asarray(x, np.float32).astype(ml_dtypes.bfloat16).astype(np.float64), axis, -1)
    blocks = v.reshape(v.shape[:-1] + (-1, 32))
    amax = np.abs(blocks).max(-1, keepdims=True)
    byte = np.maximum(np.where(amax > 0, np.frexp(amax)[1] - 1 + 127, 0) - down, 1)
    scale = np.exp2(byte - 127.0)
    codes = (blocks / scale).astype(np.float32).astype(dtype).astype(np.float64)
    return np.moveaxis((codes * scale).reshape(v.shape), -1, axis)


BF16 = ml_dtypes.bfloat16


def bf(x):
    return np.asarray(x, np.float32).astype(BF16)


def f64(x):
    return np.asarray(x).astype(np.float64)


B, T, H, HD, C = 8, 512, 1, 1024, 64
P = 8


def sigmoid(v):
    return 1.0 / (1.0 + np.exp(-v))


def palace_mask(w):
    idx = np.arange(T) % P
    intra = idx[:, None] == idx[None, :]
    return np.where(intra, 1.0, sigmoid(w))


def setup_inputs():
    c = np.repeat(np.random.standard_normal((B, T // C, H * HD)), C, axis=1)
    z = np.random.standard_normal((B, T, H * HD))
    x = np.sqrt(6.0 / np.sqrt(HD)) * c + np.sqrt(2.0 / np.sqrt(HD)) * z
    return {"x": bf(x), "inter_palace_weight": bf(0.6 + 0.2 * np.random.standard_normal(1))}


def reference(x, inter_palace_weight):
    q = f64(x).reshape(B, T, H, HD).transpose(0, 2, 1, 3)
    scores = (q @ q.transpose(0, 1, 3, 2)) * HD ** -0.5
    s = scores * palace_mask(f64(inter_palace_weight))
    e = np.exp(s - s.max(-1, keepdims=True))
    out = (mxq(e, 3, "e4m3") @ mxq(q, 2, "e4m3")) / e.sum(-1, keepdims=True)
    return out.transpose(0, 2, 1, 3).reshape(B, T, H * HD)

@@ -1,0 +1,178 @@
+from contextlib import ExitStack
+
+import concourse.mybir as mybir
+from concourse.masks import make_identity
+
+F32 = mybir.dt.float32
+BF16 = mybir.dt.bfloat16
+U32 = mybir.dt.uint32
+U8 = mybir.dt.uint8
+FP8X4 = mybir.dt.float8_e4m3fn_x4
+ALU = mybir.AluOpType
+ACT = mybir.ActivationFunctionType
+AX = mybir.AxisListType
+
+B, T, HD = 8, 512, 1024
+P = 128
+NT = T // P
+SCALE = HD ** -0.5
+FLOPS = 2 * B * T * T * HD * 2
+
+
+def tile_palaceattention_t_kernel(tc, x, inter_palace_weight, out):
+    nc = tc.nc
+    with ExitStack() as ctx:
+        const = ctx.enter_context(tc.tile_pool(name="const", bufs=1))
+        xpool = ctx.enter_context(tc.tile_pool(name="xpool", bufs=1))
+        qtp = ctx.enter_context(tc.tile_pool(name="qtp", bufs=2))
+        gqp = ctx.enter_context(tc.tile_pool(name="gqp", bufs=2))
+        qcp = ctx.enter_context(tc.tile_pool(name="qcp", bufs=2))
+        sp = ctx.enter_context(tc.tile_pool(name="sp", bufs=3))
+        ep = ctx.enter_context(tc.tile_pool(name="ep", bufs=4))
+        gep = ctx.enter_context(tc.tile_pool(name="gep", bufs=3))
+        ecp = ctx.enter_context(tc.tile_pool(name="ecp", bufs=3))
+        opool = ctx.enter_context(tc.tile_pool(name="opool", bufs=4))
+        small = ctx.enter_context(tc.tile_pool(name="small", bufs=8))
+        ps_t = ctx.enter_context(tc.psum_pool(name="ps_t", bufs=2))
+        ps_s = ctx.enter_context(tc.psum_pool(name="ps_s", bufs=2))
+        ps_e = ctx.enter_context(tc.psum_pool(name="ps_e", bufs=2))
+        ps_o = ctx.enter_context(tc.psum_pool(name="ps_o", bufs=2))
+
+        xq = []
+        for b in range(B):
+            xb = xpool.tile([P, NT, HD], BF16, name="xq%d" % b)
+            src = x[b].rearrange("(p t) h -> p t h", t=NT)
+            if b == 0:
+                for t in range(NT):
+                    nc.sync.dma_start(out=xb[:, t, :], in_=src[:, t, :])
+            else:
+                nc.sync.dma_start(out=xb[:], in_=src)
+            xq.append(xb)
+        w_bf = const.tile([P, 1], BF16)
+        nc.scalar.dma_start(out=w_bf[:], in_=inter_palace_weight.partition_broadcast(P))
+
+        ident_f = const.tile([P, P], F32)
+        make_identity(nc, ident_f[:])
+        ident_b = const.tile([P, P], BF16)
+        make_identity(nc, ident_b[:])
+        en = const.tile([P, 1], F32)
+        nc.scalar.activation(out=en[:], in_=w_bf[:], func=ACT.Exp, scale=-1.0)
+        den = const.tile([P, 1], F32)
+        nc.vector.tensor_scalar_add(out=den[:], in0=en[:], scalar1=1.0)
+        sig = const.tile([P, 1], F32)
+        nc.vector.reciprocal(out=sig[:], in_=den[:])
+        sigp = const.tile([P, 1], F32)
+        nc.vector.tensor_scalar_mul(out=sigp[:], in0=sig[:], scalar1=SCALE)
+        diff = const.tile([P, 1], F32)
+        nc.vector.tensor_scalar(out=diff[:], in0=sigp[:], scalar1=-1.0, scalar2=SCALE,
+                                op0=ALU.mult, op1=ALU.add)
+        par = const.tile([P, 2], F32)
+        nc.vector.tensor_reduce(out=par[:], in_=ident_f[:].rearrange("p (c e) -> p e c", e=2),
+                                axis=AX.X, op=ALU.add)
+        sv = const.tile([P, 2], F32)
+        nc.vector.tensor_scalar(out=sv[:], in0=par[:], scalar1=diff[:, 0:1], scalar2=sigp[:, 0:1],
+                                op0=ALU.mult, op1=ALU.add)
+        MWW = 2 * T - P
+        mw = const.tile([P, MWW], F32)
+        nc.vector.tensor_copy(out=mw[:], in_=sigp[:, 0:1].to_broadcast([P, MWW]))
+        nc.vector.tensor_copy(
+            out=mw[:, T - P:T].rearrange("p (c e) -> p c e", e=2),
+            in_=sv[:].unsqueeze(1).to_broadcast([P, P // 2, 2]),
+        )
+
+        qt, gq, qc, qs = {}, {}, {}, {}
+        e_t, rinv_t, ec_t, es_t = {}, {}, {}, {}
+        QW = HD // NT
+
+        def prep_quarter(b, c):
+            if c == 0:
+                qt_new = qtp.tile([P, NT, T], F32, name="qt")
+                gq_new = gqp.tile([P, HD, NT], BF16, name="gq", align_bytes=64)
+                qc_new = qcp.tile([P, HD], U32, name="qc", align_bytes=64)
+                qs_new = qcp.tile([P, HD], U8, name="qs", align_bytes=64)
+                qt[b], gq[b], qc[b], qs[b] = qt_new, gq_new, qc_new, qs_new
+            xf = xq[b][:].bitcast(F32)
+            tp = ps_t.tile([P, NT, P], F32)
+            for t in range(NT):
+                nc.tensor.transpose(tp[:, t, :], xf[:, t, c * P:(c + 1) * P], ident_f[:])
+            nc.scalar.copy(out=qt[b][:, c, :], in_=tp[:].rearrange("p t k -> p (t k)"))
+            h0 = c * QW
+            nc.vector.tensor_copy(
+                out=gq[b][:, h0:h0 + QW, :].rearrange("p (c i) t -> p c t i", i=4),
+                in_=xq[b][:, :, h0:h0 + QW].rearrange("p t (c i) -> p c t i", i=4),
+            )
+
+        def quant_quarter(b, c):
+            h0 = c * QW
+            nc.vector.quantize_mx(
+                out=qc[b][:, h0:h0 + QW].bitcast(FP8X4),
+                scales=qs[b][:, h0:h0 + QW],
+                in_=gq[b][:, h0:h0 + QW, :].rearrange("p h t -> p (h t)"),
+            )
+
+        def scores(g):
+            b, it = divmod(g, NT)
+            qv = qt[b][:].bitcast(BF16).rearrange("p c (k e) -> p c k e", e=2)
+            s_ps = ps_s.tile([P, T], F32)
+            for k in range(8):
+                c, e2 = divmod(k, 2)
+                nc.tensor.matmul(s_ps[:], lhsT=qv[:, c, it * P:(it + 1) * P, e2], rhs=qv[:, c, :, e2],
+                                 start=(k == 0), stop=(k == 7))
+            s = sp.tile([P, T], F32)
+            nc.vector.tensor_tensor(out=s[:], in0=s_ps[:], in1=mw[:, T - P - it * P:2 * T - P - it * P],
+                                    op=ALU.mult)
+            negm = small.tile([P, 1], F32)
+            nc.vector.tensor_reduce(out=negm[:], in_=s[:], axis=AX.X, op=ALU.max, negate=True)
+            e = ep.tile([P, T], BF16)
+            rs = small.tile([P, 1], F32)
+            nc.scalar.activation(out=e[:], in_=s[:], func=ACT.Exp, bias=negm[:, 0:1], scale=1.0,
+                                 accum_out=rs[:, 0:1])
+            rinv = small.tile([P, 1], F32)
+            nc.vector.reciprocal(out=rinv[:], in_=rs[:])
+            e_t[g], rinv_t[g] = e, rinv
+
+        def trans_e(g):
+            e = e_t[g]
+            tpe = ps_e.tile([P, NT, P], BF16)
+            for t in range(NT):
+                nc.tensor.transpose(tpe[:, t, :], e[:, t * P:(t + 1) * P], ident_b[:])
+            ge = gep.tile([P, P, NT], BF16, align_bytes=64)
+            nc.vector.tensor_copy(out=ge[:], in_=tpe[:].rearrange("q t i -> q i t"))
+            ec = ecp.tile([P, P], U32, align_bytes=64)
+            es = ecp.tile([P, P], U8, align_bytes=64)
+            nc.vector.quantize_mx(out=ec[:].bitcast(FP8X4), scales=es[:],
+                                  in_=ge[:].rearrange("q i t -> q (i t)"))
+            ec_t[g], es_t[g] = ec, es
+
+        def pv(g):
+            b, it = divmod(g, NT)
+            o_sb = opool.tile([P, HD], F32)
+            for hh in range(2):
+                cols = slice(hh * 512, (hh + 1) * 512)
+                o_ps = ps_o.tile([P, 512], F32)
+                nc.tensor.matmul_mx(out=o_ps[:], lhsT=ec_t[g][:].bitcast(FP8X4), lhsT_scale=es_t[g][:],
+                                    rhs=qc[b][:, cols].bitcast(FP8X4), rhs_scale=qs[b][:, cols],
+                                    start=True, stop=True)
+                nc.scalar.activation(out=o_sb[:, cols], in_=o_ps[:], func=ACT.Copy,
+                                     scale=rinv_t[g][:, 0:1])
+            nc.sync.dma_start(out=out[b].rearrange("(p t) h -> p t h", t=NT)[:, it, :], in_=o_sb[:])
+
+        for c in range(NT):
+            prep_quarter(0, c)
+            if c > 0:
+                quant_quarter(0, c - 1)
+        quant_quarter(0, NT - 1)
+
+        G = B * NT
+        for g in range(G + 3):
+            b, it = divmod(g, NT)
+            if g < G:
+                scores(g)
+                if b + 1 < B:
+                    prep_quarter(b + 1, it)
+            if 0 <= g - 2 < G:
+                trans_e(g - 2)
+            if g < G and b + 1 < B:
+                quant_quarter(b + 1, it)
+            if 0 <= g - 3 < G:
+                pv(g - 3)

@@ -15,8 +15,10 @@ AX = mybir.AxisListType
 B, T, HD = 8, 512, 1024
 P = 128
 NT = T // P
+G = B * NT
 SCALE = HD ** -0.5
 FLOPS = 2 * B * T * T * HD * 2
+PIN = True
 
 
 def tile_palaceattention_t_kernel(tc, x, inter_palace_weight, out):
@@ -26,9 +28,9 @@ def tile_palaceattention_t_kernel(tc, x, inter_palace_weight, out):
         xpool = ctx.enter_context(tc.tile_pool(name="xpool", bufs=1))
         qtp = ctx.enter_context(tc.tile_pool(name="qtp", bufs=2))
         gqp = ctx.enter_context(tc.tile_pool(name="gqp", bufs=2))
-        qcp = ctx.enter_context(tc.tile_pool(name="qcp", bufs=2))
-        sp = ctx.enter_context(tc.tile_pool(name="sp", bufs=3))
-        ep = ctx.enter_context(tc.tile_pool(name="ep", bufs=4))
+        qcp = ctx.enter_context(tc.tile_pool(name="qcp", bufs=3))
+        sp = ctx.enter_context(tc.tile_pool(name="sp", bufs=6))
+        ep = ctx.enter_context(tc.tile_pool(name="ep", bufs=3))
         gep = ctx.enter_context(tc.tile_pool(name="gep", bufs=3))
         ecp = ctx.enter_context(tc.tile_pool(name="ecp", bufs=3))
         opool = ctx.enter_context(tc.tile_pool(name="opool", bufs=4))
@@ -37,6 +39,8 @@ def tile_palaceattention_t_kernel(tc, x, inter_palace_weight, out):
         ps_s = ctx.enter_context(tc.psum_pool(name="ps_s", bufs=2))
         ps_e = ctx.enter_context(tc.psum_pool(name="ps_e", bufs=2))
         ps_o = ctx.enter_context(tc.psum_pool(name="ps_o", bufs=2))
+        if PIN:
+            ctx.enter_context(tc.manual_schedule())
 
         xq = []
         for b in range(B):
@@ -72,19 +76,24 @@ def tile_palaceattention_t_kernel(tc, x, inter_palace_weight, out):
         sv = const.tile([P, 2], F32)
         nc.vector.tensor_scalar(out=sv[:], in0=par[:], scalar1=diff[:, 0:1], scalar2=sigp[:, 0:1],
                                 op0=ALU.mult, op1=ALU.add)
-        MWW = 2 * T - P
-        mw = const.tile([P, MWW], F32)
-        nc.vector.tensor_copy(out=mw[:], in_=sigp[:, 0:1].to_broadcast([P, MWW]))
-        nc.vector.tensor_copy(
-            out=mw[:, T - P:T].rearrange("p (c e) -> p c e", e=2),
-            in_=sv[:].unsqueeze(1).to_broadcast([P, P // 2, 2]),
-        )
+        mk = const.tile([P, NT, T], F32)
+        for it in range(NT):
+            if it > 0:
+                nc.vector.memset(mk[:, it, 0:it * P], 1.0)
+            nc.vector.tensor_copy(
+                out=mk[:, it, it * P:(it + 1) * P].rearrange("p (c e) -> p c e", e=2),
+                in_=sv[:].unsqueeze(1).to_broadcast([P, P // 2, 2]),
+            )
+            if it < NT - 1:
+                nc.vector.tensor_copy(out=mk[:, it, (it + 1) * P:T],
+                                      in_=sigp[:, 0:1].to_broadcast([P, T - (it + 1) * P]))
 
-        qt, gq, qc, qs = {}, {}, {}, {}
-        e_t, rinv_t, ec_t, es_t = {}, {}, {}, {}
+        qt, gq, qc, qs, tp_t = {}, {}, {}, {}, {}
+        sps_t, s_t, negm_t, rs_t, e_t, rinv_t = {}, {}, {}, {}, {}, {}
+        tpe_t, ge_t, ec_t, es_t = {}, {}, {}, {}
         QW = HD // NT
 
-        def prep_quarter(b, c):
+        def tq_ops(b, c):
             if c == 0:
                 qt_new = qtp.tile([P, NT, T], F32, name="qt")
                 gq_new = gqp.tile([P, HD, NT], BF16, name="gq", align_bytes=64)
@@ -92,17 +101,24 @@ def tile_palaceattention_t_kernel(tc, x, inter_palace_weight, out):
                 qs_new = qcp.tile([P, HD], U8, name="qs", align_bytes=64)
                 qt[b], gq[b], qc[b], qs[b] = qt_new, gq_new, qc_new, qs_new
             xf = xq[b][:].bitcast(F32)
-            tp = ps_t.tile([P, NT, P], F32)
-            for t in range(NT):
-                nc.tensor.transpose(tp[:, t, :], xf[:, t, c * P:(c + 1) * P], ident_f[:])
-            nc.scalar.copy(out=qt[b][:, c, :], in_=tp[:].rearrange("p t k -> p (t k)"))
+            tp = ps_t.tile([P, NT, P], F32, name="tp")
+            tp_t[(b, c)] = tp
+            return [
+                (lambda t=t: nc.tensor.transpose(tp[:, t, :], xf[:, t, c * P:(c + 1) * P], ident_f[:]))
+                for t in range(NT)
+            ]
+
+        def qt_exit(b, c):
+            nc.scalar.copy(out=qt[b][:, c, :], in_=tp_t[(b, c)][:].rearrange("p t k -> p (t k)"))
+
+        def regroup(b, c):
             h0 = c * QW
             nc.vector.tensor_copy(
                 out=gq[b][:, h0:h0 + QW, :].rearrange("p (c i) t -> p c t i", i=4),
                 in_=xq[b][:, :, h0:h0 + QW].rearrange("p t (c i) -> p c t i", i=4),
             )
 
-        def quant_quarter(b, c):
+        def quant_q(b, c):
             h0 = c * QW
             nc.vector.quantize_mx(
                 out=qc[b][:, h0:h0 + QW].bitcast(FP8X4),
@@ -110,69 +126,123 @@ def tile_palaceattention_t_kernel(tc, x, inter_palace_weight, out):
                 in_=gq[b][:, h0:h0 + QW, :].rearrange("p h t -> p (h t)"),
             )
 
-        def scores(g):
+        def mm_ops(g):
             b, it = divmod(g, NT)
             qv = qt[b][:].bitcast(BF16).rearrange("p c (k e) -> p c k e", e=2)
-            s_ps = ps_s.tile([P, T], F32)
-            for k in range(8):
-                c, e2 = divmod(k, 2)
-                nc.tensor.matmul(s_ps[:], lhsT=qv[:, c, it * P:(it + 1) * P, e2], rhs=qv[:, c, :, e2],
-                                 start=(k == 0), stop=(k == 7))
-            s = sp.tile([P, T], F32)
-            nc.vector.tensor_tensor(out=s[:], in0=s_ps[:], in1=mw[:, T - P - it * P:2 * T - P - it * P],
-                                    op=ALU.mult)
-            negm = small.tile([P, 1], F32)
-            nc.vector.tensor_reduce(out=negm[:], in_=s[:], axis=AX.X, op=ALU.max, negate=True)
-            e = ep.tile([P, T], BF16)
-            rs = small.tile([P, 1], F32)
-            nc.scalar.activation(out=e[:], in_=s[:], func=ACT.Exp, bias=negm[:, 0:1], scale=1.0,
-                                 accum_out=rs[:, 0:1])
-            rinv = small.tile([P, 1], F32)
-            nc.vector.reciprocal(out=rinv[:], in_=rs[:])
-            e_t[g], rinv_t[g] = e, rinv
+            s_ps = ps_s.tile([P, T], F32, name="s_ps")
+            sps_t[g] = s_ps
+            return [
+                (lambda k=k: nc.tensor.matmul(
+                    s_ps[:, it * P:T], lhsT=qv[:, k // 2, it * P:(it + 1) * P, k % 2],
+                    rhs=qv[:, k // 2, it * P:T, k % 2], start=(k == 0), stop=(k == 7)))
+                for k in range(8)
+            ]
 
-        def trans_e(g):
+        def ts(g):
+            b, it = divmod(g, NT)
+            for jt in range(it):
+                nc.tensor.transpose(sps_t[g][:, jt * P:(jt + 1) * P],
+                                    s_t[b * NT + jt][:, it * P:(it + 1) * P], ident_f[:])
+
+        def stats(g):
+            it = g % NT
+            s = sp.tile([P, T], F32, name="s")
+            nc.vector.tensor_tensor(out=s[:], in0=sps_t[g][:], in1=mk[:, it, :], op=ALU.mult)
+            negm = small.tile([P, 1], F32, name="negm")
+            nc.vector.tensor_reduce(out=negm[:], in_=s[:], axis=AX.X, op=ALU.max, negate=True)
+            s_t[g], negm_t[g] = s, negm
+
+        def expo(g):
+            e = ep.tile([P, T], BF16, name="e")
+            rs = small.tile([P, 1], F32, name="rs")
+            nc.scalar.activation(out=e[:], in_=s_t[g][:], func=ACT.Exp, bias=negm_t[g][:, 0:1], scale=1.0,
+                                 accum_out=rs[:, 0:1])
+            e_t[g], rs_t[g] = e, rs
+
+        def recip(g):
+            rinv = small.tile([P, 1], F32, name="rinv")
+            nc.vector.reciprocal(out=rinv[:], in_=rs_t[g][:])
+            rinv_t[g] = rinv
+
+        def te_ops(g):
             e = e_t[g]
-            tpe = ps_e.tile([P, NT, P], BF16)
-            for t in range(NT):
-                nc.tensor.transpose(tpe[:, t, :], e[:, t * P:(t + 1) * P], ident_b[:])
-            ge = gep.tile([P, P, NT], BF16, align_bytes=64)
-            nc.vector.tensor_copy(out=ge[:], in_=tpe[:].rearrange("q t i -> q i t"))
-            ec = ecp.tile([P, P], U32, align_bytes=64)
-            es = ecp.tile([P, P], U8, align_bytes=64)
+            tpe = ps_e.tile([P, NT, P], BF16, name="tpe")
+            tpe_t[g] = tpe
+            return [
+                (lambda t=t: nc.tensor.transpose(tpe[:, t, :], e[:, t * P:(t + 1) * P], ident_b[:]))
+                for t in range(NT)
+            ]
+
+        def e_exit(g):
+            ge = gep.tile([P, P, NT], BF16, name="ge", align_bytes=64)
+            nc.vector.tensor_copy(out=ge[:], in_=tpe_t[g][:].rearrange("q t i -> q i t"))
+            ge_t[g] = ge
+
+        def quant_e(g):
+            ec = ecp.tile([P, P], U32, name="ec", align_bytes=64)
+            es = ecp.tile([P, P], U8, name="es", align_bytes=64)
             nc.vector.quantize_mx(out=ec[:].bitcast(FP8X4), scales=es[:],
-                                  in_=ge[:].rearrange("q i t -> q (i t)"))
+                                  in_=ge_t[g][:].rearrange("q i t -> q (i t)"))
             ec_t[g], es_t[g] = ec, es
 
         def pv(g):
             b, it = divmod(g, NT)
-            o_sb = opool.tile([P, HD], F32)
+            o_sb = opool.tile([P, HD], F32, name="o_sb")
+            o_pss = []
             for hh in range(2):
                 cols = slice(hh * 512, (hh + 1) * 512)
-                o_ps = ps_o.tile([P, 512], F32)
+                o_ps = ps_o.tile([P, 512], F32, name="o_ps")
                 nc.tensor.matmul_mx(out=o_ps[:], lhsT=ec_t[g][:].bitcast(FP8X4), lhsT_scale=es_t[g][:],
                                     rhs=qc[b][:, cols].bitcast(FP8X4), rhs_scale=qs[b][:, cols],
                                     start=True, stop=True)
-                nc.scalar.activation(out=o_sb[:, cols], in_=o_ps[:], func=ACT.Copy,
+                o_pss.append(o_ps)
+            for hh in range(2):
+                cols = slice(hh * 512, (hh + 1) * 512)
+                nc.scalar.activation(out=o_sb[:, cols], in_=o_pss[hh][:], func=ACT.Copy,
                                      scale=rinv_t[g][:, 0:1])
             nc.sync.dma_start(out=out[b].rearrange("(p t) h -> p t h", t=NT)[:, it, :], in_=o_sb[:])
 
-        for c in range(NT):
-            prep_quarter(0, c)
-            if c > 0:
-                quant_quarter(0, c - 1)
-        quant_quarter(0, NT - 1)
+        def weave(mms, trs):
+            n = max(len(mms), len(trs))
+            for i in range(n):
+                if i < len(mms):
+                    mms[i]()
+                if i < len(trs):
+                    trs[i]()
 
-        G = B * NT
+        for c in range(NT):
+            weave([], tq_ops(0, c))
+            qt_exit(0, c)
+            regroup(0, c)
+            if c > 0:
+                quant_q(0, c - 1)
+        quant_q(0, NT - 1)
+
         for g in range(G + 3):
             b, it = divmod(g, NT)
-            if g < G:
-                scores(g)
-                if b + 1 < B:
-                    prep_quarter(b + 1, it)
-            if 0 <= g - 2 < G:
-                trans_e(g - 2)
-            if g < G and b + 1 < B:
-                quant_quarter(b + 1, it)
+            live = g < G
+            nxt = live and b + 1 < B
+            if 0 <= g - 1 < G:
+                stats(g - 1)
+            mm = mm_ops(g) if live else []
+            te = te_ops(g - 2) if 0 <= g - 2 < G else []
+            weave(mm[0:4], te)
+            if 0 <= g - 1 < G:
+                expo(g - 1)
             if 0 <= g - 3 < G:
                 pv(g - 3)
+            tq = tq_ops(b + 1, it) if nxt else []
+            weave(mm[4:8], tq)
+            if 0 <= g - 2 < G:
+                e_exit(g - 2)
+            if nxt:
+                regroup(b + 1, it)
+            if 0 <= g - 2 < G:
+                quant_e(g - 2)
+            if nxt:
+                quant_q(b + 1, it)
+                qt_exit(b + 1, it)
+            if live:
+                ts(g)
+            if 0 <= g - 1 < G:
+                recip(g - 1)

@@ -19,6 +19,7 @@ G = B * NT
 SCALE = HD ** -0.5
 FLOPS = 2 * B * T * T * HD * 2
 PIN = True
+V_EXIT_TILES = (3,)
 
 
 def tile_palaceattention_t_kernel(tc, x, inter_palace_weight, out):
@@ -27,7 +28,7 @@ def tile_palaceattention_t_kernel(tc, x, inter_palace_weight, out):
         const = ctx.enter_context(tc.tile_pool(name="const", bufs=1))
         xpool = ctx.enter_context(tc.tile_pool(name="xpool", bufs=1))
         qtp = ctx.enter_context(tc.tile_pool(name="qtp", bufs=2))
-        gqp = ctx.enter_context(tc.tile_pool(name="gqp", bufs=2))
+        gqp = ctx.enter_context(tc.tile_pool(name="gqp", bufs=1))
         qcp = ctx.enter_context(tc.tile_pool(name="qcp", bufs=3))
         sp = ctx.enter_context(tc.tile_pool(name="sp", bufs=6))
         ep = ctx.enter_context(tc.tile_pool(name="ep", bufs=3))
@@ -90,16 +91,13 @@ def tile_palaceattention_t_kernel(tc, x, inter_palace_weight, out):
 
         qt, gq, qc, qs, tp_t = {}, {}, {}, {}, {}
         sps_t, s_t, negm_t, rs_t, e_t, rinv_t = {}, {}, {}, {}, {}, {}
-        tpe_t, ge_t, ec_t, es_t = {}, {}, {}, {}
+        tpe_t, ge_t, ec_t, es_t, ops_t, osb_t = {}, {}, {}, {}, {}, {}
         QW = HD // NT
 
         def tq_ops(b, c):
             if c == 0:
                 qt_new = qtp.tile([P, NT, T], F32, name="qt")
-                gq_new = gqp.tile([P, HD, NT], BF16, name="gq", align_bytes=64)
-                qc_new = qcp.tile([P, HD], U32, name="qc", align_bytes=64)
-                qs_new = qcp.tile([P, HD], U8, name="qs", align_bytes=64)
-                qt[b], gq[b], qc[b], qs[b] = qt_new, gq_new, qc_new, qs_new
+                qt[b] = qt_new
             xf = xq[b][:].bitcast(F32)
             tp = ps_t.tile([P, NT, P], F32, name="tp")
             tp_t[(b, c)] = tp
@@ -111,19 +109,25 @@ def tile_palaceattention_t_kernel(tc, x, inter_palace_weight, out):
         def qt_exit(b, c):
             nc.scalar.copy(out=qt[b][:, c, :], in_=tp_t[(b, c)][:].rearrange("p t k -> p (t k)"))
 
-        def regroup(b, c):
+        def regroup(n):
+            b, c = divmod(n, NT)
             h0 = c * QW
-            nc.vector.tensor_copy(
-                out=gq[b][:, h0:h0 + QW, :].rearrange("p (c i) t -> p c t i", i=4),
-                in_=xq[b][:, :, h0:h0 + QW].rearrange("p t (c i) -> p c t i", i=4),
-            )
+            gq_new = gqp.tile([P, QW, NT], BF16, name="gq", align_bytes=64)
+            gq[n] = gq_new
+            nc.gpsimd.tensor_scalar(out=gq_new[:], in0=xq[b][:, :, h0:h0 + QW].rearrange("p t h -> p h t"),
+                                    scalar1=1.0, scalar2=0.0, op0=ALU.mult, op1=ALU.add)
 
-        def quant_q(b, c):
+        def quant_q(n):
+            b, c = divmod(n, NT)
+            if c == 0:
+                qc_new = qcp.tile([P, HD], U32, name="qc", align_bytes=64)
+                qs_new = qcp.tile([P, HD], U8, name="qs", align_bytes=64)
+                qc[b], qs[b] = qc_new, qs_new
             h0 = c * QW
             nc.vector.quantize_mx(
                 out=qc[b][:, h0:h0 + QW].bitcast(FP8X4),
                 scales=qs[b][:, h0:h0 + QW],
-                in_=gq[b][:, h0:h0 + QW, :].rearrange("p h t -> p (h t)"),
+                in_=gq[n][:].rearrange("p h t -> p (h t)"),
             )
 
         def mm_ops(g):
@@ -144,13 +148,15 @@ def tile_palaceattention_t_kernel(tc, x, inter_palace_weight, out):
                 nc.tensor.transpose(sps_t[g][:, jt * P:(jt + 1) * P],
                                     s_t[b * NT + jt][:, it * P:(it + 1) * P], ident_f[:])
 
-        def stats(g):
-            it = g % NT
+        def mask(g):
             s = sp.tile([P, T], F32, name="s")
-            nc.vector.tensor_tensor(out=s[:], in0=sps_t[g][:], in1=mk[:, it, :], op=ALU.mult)
+            nc.vector.tensor_tensor(out=s[:], in0=sps_t[g][:], in1=mk[:, g % NT, :], op=ALU.mult)
+            s_t[g] = s
+
+        def rowmax(g):
             negm = small.tile([P, 1], F32, name="negm")
-            nc.vector.tensor_reduce(out=negm[:], in_=s[:], axis=AX.X, op=ALU.max, negate=True)
-            s_t[g], negm_t[g] = s, negm
+            nc.vector.tensor_reduce(out=negm[:], in_=s_t[g][:], axis=AX.X, op=ALU.max, negate=True)
+            negm_t[g] = negm
 
         def expo(g):
             e = ep.tile([P, T], BF16, name="e")
@@ -185,9 +191,8 @@ def tile_palaceattention_t_kernel(tc, x, inter_palace_weight, out):
                                   in_=ge_t[g][:].rearrange("q i t -> q (i t)"))
             ec_t[g], es_t[g] = ec, es
 
-        def pv(g):
-            b, it = divmod(g, NT)
-            o_sb = opool.tile([P, HD], F32, name="o_sb")
+        def mx(g):
+            b = g // NT
             o_pss = []
             for hh in range(2):
                 cols = slice(hh * 512, (hh + 1) * 512)
@@ -196,53 +201,79 @@ def tile_palaceattention_t_kernel(tc, x, inter_palace_weight, out):
                                     rhs=qc[b][:, cols].bitcast(FP8X4), rhs_scale=qs[b][:, cols],
                                     start=True, stop=True)
                 o_pss.append(o_ps)
-            for hh in range(2):
-                cols = slice(hh * 512, (hh + 1) * 512)
-                nc.scalar.activation(out=o_sb[:, cols], in_=o_pss[hh][:], func=ACT.Copy,
+            ops_t[g] = o_pss
+
+        def o_half(g, hh, on_vector):
+            if hh == 0:
+                o_new = opool.tile([P, HD], F32, name="o_sb")
+                osb_t[g] = o_new
+            cols = slice(hh * 512, (hh + 1) * 512)
+            if on_vector:
+                nc.vector.tensor_scalar_mul(out=osb_t[g][:, cols], in0=ops_t[g][hh][:],
+                                            scalar1=rinv_t[g][:, 0:1])
+            else:
+                nc.scalar.activation(out=osb_t[g][:, cols], in_=ops_t[g][hh][:], func=ACT.Copy,
                                      scale=rinv_t[g][:, 0:1])
-            nc.sync.dma_start(out=out[b].rearrange("(p t) h -> p t h", t=NT)[:, it, :], in_=o_sb[:])
 
-        def weave(mms, trs):
-            n = max(len(mms), len(trs))
-            for i in range(n):
-                if i < len(mms):
-                    mms[i]()
-                if i < len(trs):
-                    trs[i]()
-
-        for c in range(NT):
-            weave([], tq_ops(0, c))
-            qt_exit(0, c)
-            regroup(0, c)
-            if c > 0:
-                quant_q(0, c - 1)
-        quant_q(0, NT - 1)
-
-        for g in range(G + 3):
+        def store(g):
             b, it = divmod(g, NT)
-            live = g < G
-            nxt = live and b + 1 < B
-            if 0 <= g - 1 < G:
-                stats(g - 1)
-            mm = mm_ops(g) if live else []
-            te = te_ops(g - 2) if 0 <= g - 2 < G else []
-            weave(mm[0:4], te)
-            if 0 <= g - 1 < G:
-                expo(g - 1)
-            if 0 <= g - 3 < G:
-                pv(g - 3)
-            tq = tq_ops(b + 1, it) if nxt else []
-            weave(mm[4:8], tq)
-            if 0 <= g - 2 < G:
-                e_exit(g - 2)
-            if nxt:
-                regroup(b + 1, it)
-            if 0 <= g - 2 < G:
-                quant_e(g - 2)
-            if nxt:
-                quant_q(b + 1, it)
-                qt_exit(b + 1, it)
-            if live:
+            nc.sync.dma_start(out=out[b].rearrange("(p t) h -> p t h", t=NT)[:, it, :], in_=osb_t[g][:])
+
+        def weave(mms, trs, per):
+            j = 0
+            for m in mms:
+                m()
+                for r in trs[j:j + per]:
+                    r()
+                j += per
+            for r in trs[j:]:
+                r()
+
+        def ok(i):
+            return 0 <= i < G
+
+        for m in range(NT + 1):
+            weave([], tq_ops(m // NT, m % NT), 1)
+            qt_exit(m // NT, m % NT)
+        regroup(0)
+        quant_q(0)
+        regroup(1)
+        weave(mm_ops(0), [], 1)
+
+        for g in range(G + 4):
+            m = g + NT + 1
+            if ok(g - 1):
+                mask(g - 1)
+            if ok(g):
                 ts(g)
-            if 0 <= g - 1 < G:
-                recip(g - 1)
+            if ok(g - 2):
+                weave([], te_ops(g - 2), 1)
+            if ok(g - 1):
+                rowmax(g - 1)
+            if ok(g - 4) and (g - 4) % NT in V_EXIT_TILES:
+                o_half(g - 4, 1, True)
+                store(g - 4)
+            if ok(g - 3):
+                quant_e(g - 3)
+            if g + 1 < G:
+                quant_q(g + 1)
+            if g + 2 < G:
+                regroup(g + 2)
+            mm = mm_ops(g + 1) if ok(g + 1) else []
+            tq = tq_ops(m // NT, m % NT) if m < G else []
+            weave(mm[0:4], [], 1)
+            if ok(g - 3):
+                mx(g - 3)
+            weave(mm[4:8], tq, 1)
+            if ok(g - 1):
+                expo(g - 1)
+            if ok(g - 3):
+                o_half(g - 3, 0, False)
+                if (g - 3) % NT not in V_EXIT_TILES:
+                    o_half(g - 3, 1, False)
+                    store(g - 3)
+            if m < G:
+                qt_exit(m // NT, m % NT)
+            if ok(g - 2):
+                e_exit(g - 2)
+                recip(g - 2)

@@ -19,7 +19,7 @@ G = B * NT
 SCALE = HD ** -0.5
 FLOPS = 2 * B * T * T * HD * 2
 PIN = True
-V_EXIT_TILES = (3,)
+V_EXIT_TILES = ()
 
 
 def tile_palaceattention_t_kernel(tc, x, inter_palace_weight, out):

@@ -19,7 +19,6 @@ G = B * NT
 SCALE = HD ** -0.5
 FLOPS = 2 * B * T * T * HD * 2
 PIN = True
-V_EXIT_TILES = ()
 
 
 def tile_palaceattention_t_kernel(tc, x, inter_palace_weight, out):
@@ -48,8 +47,9 @@ def tile_palaceattention_t_kernel(tc, x, inter_palace_weight, out):
             xb = xpool.tile([P, NT, HD], BF16, name="xq%d" % b)
             src = x[b].rearrange("(p t) h -> p t h", t=NT)
             if b == 0:
-                for t in range(NT):
-                    nc.sync.dma_start(out=xb[:, t, :], in_=src[:, t, :])
+                for c in range(NT):
+                    cols = slice(c * (HD // NT), (c + 1) * (HD // NT))
+                    nc.sync.dma_start(out=xb[:, :, cols], in_=src[:, :, cols])
             else:
                 nc.sync.dma_start(out=xb[:], in_=src)
             xq.append(xb)
@@ -181,7 +181,7 @@ def tile_palaceattention_t_kernel(tc, x, inter_palace_weight, out):
 
         def e_exit(g):
             ge = gep.tile([P, P, NT], BF16, name="ge", align_bytes=64)
-            nc.vector.tensor_copy(out=ge[:], in_=tpe_t[g][:].rearrange("q t i -> q i t"))
+            nc.scalar.copy(out=ge[:], in_=tpe_t[g][:].rearrange("q t i -> q i t"))
             ge_t[g] = ge
 
         def quant_e(g):
@@ -232,15 +232,21 @@ def tile_palaceattention_t_kernel(tc, x, inter_palace_weight, out):
         def ok(i):
             return 0 <= i < G
 
-        for m in range(NT + 1):
-            weave([], tq_ops(m // NT, m % NT), 1)
-            qt_exit(m // NT, m % NT)
-        regroup(0)
+        for c in range(NT):
+            weave([], tq_ops(0, c), 1)
+            qt_exit(0, c)
+            if c == 0:
+                regroup(0)
+                mm = mm_ops(0)
+            else:
+                weave(mm[2 * c - 2:2 * c], [], 1)
+        weave(mm[6:8], [], 1)
         quant_q(0)
         regroup(1)
-        weave(mm_ops(0), [], 1)
+        weave([], tq_ops(1, 0), 1)
+        qt_exit(1, 0)
 
-        for g in range(G + 4):
+        for g in range(G + 5):
             m = g + NT + 1
             if ok(g - 1):
                 mask(g - 1)
@@ -250,7 +256,7 @@ def tile_palaceattention_t_kernel(tc, x, inter_palace_weight, out):
                 weave([], te_ops(g - 2), 1)
             if ok(g - 1):
                 rowmax(g - 1)
-            if ok(g - 4) and (g - 4) % NT in V_EXIT_TILES:
+            if ok(g - 4):
                 o_half(g - 4, 1, True)
                 store(g - 4)
             if ok(g - 3):
@@ -267,13 +273,11 @@ def tile_palaceattention_t_kernel(tc, x, inter_palace_weight, out):
             weave(mm[4:8], tq, 1)
             if ok(g - 1):
                 expo(g - 1)
+            if ok(g - 2):
+                e_exit(g - 2)
             if ok(g - 3):
                 o_half(g - 3, 0, False)
-                if (g - 3) % NT not in V_EXIT_TILES:
-                    o_half(g - 3, 1, False)
-                    store(g - 3)
             if m < G:
                 qt_exit(m // NT, m % NT)
             if ok(g - 2):
-                e_exit(g - 2)
                 recip(g - 2)

@@ -215,9 +215,10 @@ def tile_palaceattention_t_kernel(tc, x, inter_palace_weight, out):
                 nc.scalar.activation(out=osb_t[g][:, cols], in_=ops_t[g][hh][:], func=ACT.Copy,
                                      scale=rinv_t[g][:, 0:1])
 
-        def store(g):
+        def store(g, hh):
             b, it = divmod(g, NT)
-            nc.sync.dma_start(out=out[b].rearrange("(p t) h -> p t h", t=NT)[:, it, :], in_=osb_t[g][:])
+            cols = slice(hh * 512, (hh + 1) * 512)
+            nc.sync.dma_start(out=out[b].rearrange("(p t) h -> p t h", t=NT)[:, it, cols], in_=osb_t[g][:, cols])
 
         def weave(mms, trs, per):
             j = 0
@@ -248,25 +249,32 @@ def tile_palaceattention_t_kernel(tc, x, inter_palace_weight, out):
 
         for g in range(G + 5):
             m = g + NT + 1
+            wide = (g + 1) % NT < 2
             if ok(g - 1):
                 mask(g - 1)
             if ok(g):
                 ts(g)
             if ok(g - 2):
                 weave([], te_ops(g - 2), 1)
+            tq = tq_ops(m // NT, m % NT) if m < G else []
+            if not wide:
+                weave([], tq, 1)
+                tq = []
             if ok(g - 1):
                 rowmax(g - 1)
-            if ok(g - 4):
+            if ok(g - 4) and g < G:
                 o_half(g - 4, 1, True)
-                store(g - 4)
+                store(g - 4, 1)
             if ok(g - 3):
                 quant_e(g - 3)
             if g + 1 < G:
                 quant_q(g + 1)
             if g + 2 < G:
                 regroup(g + 2)
+            if ok(g - 4) and g >= G:
+                o_half(g - 4, 1, True)
+                store(g - 4, 1)
             mm = mm_ops(g + 1) if ok(g + 1) else []
-            tq = tq_ops(m // NT, m % NT) if m < G else []
             weave(mm[0:4], [], 1)
             if ok(g - 3):
                 mx(g - 3)
@@ -277,6 +285,7 @@ def tile_palaceattention_t_kernel(tc, x, inter_palace_weight, out):
                 e_exit(g - 2)
             if ok(g - 3):
                 o_half(g - 3, 0, False)
+                store(g - 3, 0)
             if m < G:
                 qt_exit(m // NT, m % NT)
             if ok(g - 2):

@@ -215,10 +215,9 @@ def tile_palaceattention_t_kernel(tc, x, inter_palace_weight, out):
                 nc.scalar.activation(out=osb_t[g][:, cols], in_=ops_t[g][hh][:], func=ACT.Copy,
                                      scale=rinv_t[g][:, 0:1])
 
-        def store(g, hh):
+        def store(g):
             b, it = divmod(g, NT)
-            cols = slice(hh * 512, (hh + 1) * 512)
-            nc.sync.dma_start(out=out[b].rearrange("(p t) h -> p t h", t=NT)[:, it, cols], in_=osb_t[g][:, cols])
+            nc.sync.dma_start(out=out[b].rearrange("(p t) h -> p t h", t=NT)[:, it, :], in_=osb_t[g][:])
 
         def weave(mms, trs, per):
             j = 0
@@ -249,22 +248,17 @@ def tile_palaceattention_t_kernel(tc, x, inter_palace_weight, out):
 
         for g in range(G + 5):
             m = g + NT + 1
-            wide = (g + 1) % NT < 2
             if ok(g - 1):
                 mask(g - 1)
             if ok(g):
                 ts(g)
             if ok(g - 2):
                 weave([], te_ops(g - 2), 1)
-            tq = tq_ops(m // NT, m % NT) if m < G else []
-            if not wide:
-                weave([], tq, 1)
-                tq = []
             if ok(g - 1):
                 rowmax(g - 1)
             if ok(g - 4) and g < G:
                 o_half(g - 4, 1, True)
-                store(g - 4, 1)
+                store(g - 4)
             if ok(g - 3):
                 quant_e(g - 3)
             if g + 1 < G:
@@ -273,8 +267,9 @@ def tile_palaceattention_t_kernel(tc, x, inter_palace_weight, out):
                 regroup(g + 2)
             if ok(g - 4) and g >= G:
                 o_half(g - 4, 1, True)
-                store(g - 4, 1)
+                store(g - 4)
             mm = mm_ops(g + 1) if ok(g + 1) else []
+            tq = tq_ops(m // NT, m % NT) if m < G else []
             weave(mm[0:4], [], 1)
             if ok(g - 3):
                 mx(g - 3)
@@ -285,7 +280,6 @@ def tile_palaceattention_t_kernel(tc, x, inter_palace_weight, out):
                 e_exit(g - 2)
             if ok(g - 3):
                 o_half(g - 3, 0, False)
-                store(g - 3, 0)
             if m < G:
                 qt_exit(m // NT, m % NT)
             if ok(g - 2):

@@ -142,11 +142,13 @@ def tile_palaceattention_t_kernel(tc, x, inter_palace_weight, out):
                 for k in range(8)
             ]
 
-        def ts(g):
+        def ts_ops(g):
             b, it = divmod(g, NT)
-            for jt in range(it):
-                nc.tensor.transpose(sps_t[g][:, jt * P:(jt + 1) * P],
-                                    s_t[b * NT + jt][:, it * P:(it + 1) * P], ident_f[:])
+            return [
+                (lambda jt=jt: nc.tensor.transpose(sps_t[g][:, jt * P:(jt + 1) * P],
+                                                   s_t[b * NT + jt][:, it * P:(it + 1) * P], ident_f[:]))
+                for jt in range(it)
+            ]
 
         def mask(g):
             s = sp.tile([P, T], F32, name="s")
@@ -250,10 +252,7 @@ def tile_palaceattention_t_kernel(tc, x, inter_palace_weight, out):
             m = g + NT + 1
             if ok(g - 1):
                 mask(g - 1)
-            if ok(g):
-                ts(g)
-            if ok(g - 2):
-                weave([], te_ops(g - 2), 1)
+            tr = (ts_ops(g) if ok(g) else []) + (te_ops(g - 2) if ok(g - 2) else [])
             if ok(g - 1):
                 rowmax(g - 1)
             if ok(g - 4) and g < G:
@@ -270,7 +269,8 @@ def tile_palaceattention_t_kernel(tc, x, inter_palace_weight, out):
                 store(g - 4)
             mm = mm_ops(g + 1) if ok(g + 1) else []
             tq = tq_ops(m // NT, m % NT) if m < G else []
-            weave(mm[0:4], [], 1)
+            weave(mm[0:3], tr, 3)
+            weave(mm[3:4], [], 1)
             if ok(g - 3):
                 mx(g - 3)
             weave(mm[4:8], tq, 1)

@@ -58,8 +58,6 @@ def tile_palaceattention_t_kernel(tc, x, inter_palace_weight, out):
 
         ident_f = const.tile([P, P], F32)
         make_identity(nc, ident_f[:])
-        ident_b = const.tile([P, P], BF16)
-        make_identity(nc, ident_b[:])
         en = const.tile([P, 1], F32)
         nc.scalar.activation(out=en[:], in_=w_bf[:], func=ACT.Exp, scale=-1.0)
         den = const.tile([P, 1], F32)
@@ -163,8 +161,9 @@ def tile_palaceattention_t_kernel(tc, x, inter_palace_weight, out):
         def expo(g):
             e = ep.tile([P, T], BF16, name="e")
             rs = small.tile([P, 1], F32, name="rs")
-            nc.scalar.activation(out=e[:], in_=s_t[g][:], func=ACT.Exp, bias=negm_t[g][:, 0:1], scale=1.0,
-                                 accum_out=rs[:, 0:1])
+            nc.scalar.activation(out=e[:].rearrange("p (u k j) -> p u k j", u=2, j=2),
+                                 in_=s_t[g][:].rearrange("p (u j k) -> p u k j", u=2, j=2),
+                                 func=ACT.Exp, bias=negm_t[g][:, 0:1], scale=1.0, accum_out=rs[:, 0:1])
             e_t[g], rs_t[g] = e, rs
 
         def recip(g):
@@ -173,17 +172,18 @@ def tile_palaceattention_t_kernel(tc, x, inter_palace_weight, out):
             rinv_t[g] = rinv
 
         def te_ops(g):
-            e = e_t[g]
-            tpe = ps_e.tile([P, NT, P], BF16, name="tpe")
+            ew = e_t[g][:].bitcast(F32)
+            tpe = ps_e.tile([P, 2, P], F32, name="tpe")
             tpe_t[g] = tpe
             return [
-                (lambda t=t: nc.tensor.transpose(tpe[:, t, :], e[:, t * P:(t + 1) * P], ident_b[:]))
-                for t in range(NT)
+                (lambda u=u: nc.tensor.transpose(tpe[:, u, :], ew[:, u * P:(u + 1) * P], ident_f[:]))
+                for u in range(2)
             ]
 
         def e_exit(g):
             ge = gep.tile([P, P, NT], BF16, name="ge", align_bytes=64)
-            nc.scalar.copy(out=ge[:], in_=tpe_t[g][:].rearrange("q t i -> q i t"))
+            nc.scalar.copy(out=ge[:].rearrange("q i t -> q (i t)").bitcast(F32).rearrange("q (i u) -> q i u", u=2),
+                           in_=tpe_t[g][:].rearrange("q u i -> q i u"))
             ge_t[g] = ge
 
         def quant_e(g):

@@ -26,19 +26,19 @@ def tile_palaceattention_t_kernel(tc, x, inter_palace_weight, out):
     with ExitStack() as ctx:
         const = ctx.enter_context(tc.tile_pool(name="const", bufs=1))
         xpool = ctx.enter_context(tc.tile_pool(name="xpool", bufs=1))
-        qtp = ctx.enter_context(tc.tile_pool(name="qtp", bufs=2))
+        qtp = ctx.enter_context(tc.tile_pool(name="qtp", bufs=3))
         gqp = ctx.enter_context(tc.tile_pool(name="gqp", bufs=1))
         qcp = ctx.enter_context(tc.tile_pool(name="qcp", bufs=3))
-        sp = ctx.enter_context(tc.tile_pool(name="sp", bufs=6))
+        sp = ctx.enter_context(tc.tile_pool(name="sp", bufs=8))
         ep = ctx.enter_context(tc.tile_pool(name="ep", bufs=3))
         gep = ctx.enter_context(tc.tile_pool(name="gep", bufs=3))
         ecp = ctx.enter_context(tc.tile_pool(name="ecp", bufs=3))
         opool = ctx.enter_context(tc.tile_pool(name="opool", bufs=4))
-        small = ctx.enter_context(tc.tile_pool(name="small", bufs=8))
+        small = ctx.enter_context(tc.tile_pool(name="small", bufs=12))
         ps_t = ctx.enter_context(tc.psum_pool(name="ps_t", bufs=2))
         ps_s = ctx.enter_context(tc.psum_pool(name="ps_s", bufs=2))
-        ps_e = ctx.enter_context(tc.psum_pool(name="ps_e", bufs=2))
-        ps_o = ctx.enter_context(tc.psum_pool(name="ps_o", bufs=2))
+        ps_e = ctx.enter_context(tc.psum_pool(name="ps_e", bufs=1))
+        ps_o = ctx.enter_context(tc.psum_pool(name="ps_o", bufs=3))
         if PIN:
             ctx.enter_context(tc.manual_schedule())
 
@@ -206,7 +206,7 @@ def tile_palaceattention_t_kernel(tc, x, inter_palace_weight, out):
             ops_t[g] = o_pss
 
         def o_half(g, hh, on_vector):
-            if hh == 0:
+            if g not in osb_t:
                 o_new = opool.tile([P, HD], F32, name="o_sb")
                 osb_t[g] = o_new
             cols = slice(hh * 512, (hh + 1) * 512)
@@ -221,66 +221,59 @@ def tile_palaceattention_t_kernel(tc, x, inter_palace_weight, out):
             b, it = divmod(g, NT)
             nc.sync.dma_start(out=out[b].rearrange("(p t) h -> p t h", t=NT)[:, it, :], in_=osb_t[g][:])
 
-        def weave(mms, trs, per):
-            j = 0
-            for m in mms:
-                m()
-                for r in trs[j:j + per]:
-                    r()
-                j += per
-            for r in trs[j:]:
-                r()
+        def weave(mms, trs):
+            for i in range(max(len(mms), len(trs))):
+                for op in mms[i:i + 1] + trs[i:i + 1]:
+                    op()
 
         def ok(i):
             return 0 <= i < G
 
         for c in range(NT):
-            weave([], tq_ops(0, c), 1)
+            weave([], tq_ops(0, c))
             qt_exit(0, c)
             if c == 0:
                 regroup(0)
                 mm = mm_ops(0)
             else:
-                weave(mm[2 * c - 2:2 * c], [], 1)
-        weave(mm[6:8], [], 1)
-        quant_q(0)
-        regroup(1)
-        weave([], tq_ops(1, 0), 1)
-        qt_exit(1, 0)
+                weave(mm[2 * c - 2:2 * c], [])
+        weave(mm[6:8], tq_ops(1, 0))
+        late = [4]
 
-        for g in range(G + 5):
-            m = g + NT + 1
-            if ok(g - 1):
-                mask(g - 1)
-            tr = (ts_ops(g) if ok(g) else []) + (te_ops(g - 2) if ok(g - 2) else [])
-            if ok(g - 1):
-                rowmax(g - 1)
-            if ok(g - 4) and g < G:
-                o_half(g - 4, 1, True)
-                store(g - 4)
+        for g in range(1, G + 9):
+            ms = {1: [5, 6], 2: [7]}.get(g, [g + 5])
+            ms = [m for m in ms if m < G]
             if ok(g - 3):
-                quant_e(g - 3)
-            if g + 1 < G:
-                quant_q(g + 1)
-            if g + 2 < G:
-                regroup(g + 2)
-            if ok(g - 4) and g >= G:
-                o_half(g - 4, 1, True)
-                store(g - 4)
-            mm = mm_ops(g + 1) if ok(g + 1) else []
-            tq = tq_ops(m // NT, m % NT) if m < G else []
-            weave(mm[0:3], tr, 3)
-            weave(mm[3:4], [], 1)
-            if ok(g - 3):
-                mx(g - 3)
-            weave(mm[4:8], tq, 1)
-            if ok(g - 1):
-                expo(g - 1)
+                rowmax(g - 3)
             if ok(g - 2):
-                e_exit(g - 2)
-            if ok(g - 3):
-                o_half(g - 3, 0, False)
-            if m < G:
+                mask(g - 2)
+            if ok(g - 7):
+                quant_e(g - 7)
+            if ok(g - 1):
+                quant_q(g - 1)
+            if ok(g):
+                regroup(g)
+            if ok(g - 5):
+                recip(g - 5)
+            if ok(g - 8):
+                o_half(g - 8, 1, True)
+                store(g - 8)
+            for m in late:
                 qt_exit(m // NT, m % NT)
-            if ok(g - 2):
-                recip(g - 2)
+            if ok(g - 3):
+                expo(g - 3)
+            mm = mm_ops(g) if ok(g) else []
+            ts = ts_ops(g - 1) if ok(g - 1) else []
+            te = te_ops(g - 5) if ok(g - 5) else []
+            tq = []
+            for m in ms:
+                tq += tq_ops(m // NT, m % NT)
+            weave(mm[0:3], ts)
+            if ok(g - 7):
+                mx(g - 7)
+            weave(mm[3:8], te + tq)
+            if ok(g - 7):
+                o_half(g - 7, 0, False)
+            if ok(g - 5):
+                e_exit(g - 5)
+            late = ms

@@ -33,7 +33,7 @@ def tile_palaceattention_t_kernel(tc, x, inter_palace_weight, out):
         ep = ctx.enter_context(tc.tile_pool(name="ep", bufs=3))
         gep = ctx.enter_context(tc.tile_pool(name="gep", bufs=3))
         ecp = ctx.enter_context(tc.tile_pool(name="ecp", bufs=3))
-        opool = ctx.enter_context(tc.tile_pool(name="opool", bufs=4))
+        opool = ctx.enter_context(tc.tile_pool(name="opool", bufs=8))
         small = ctx.enter_context(tc.tile_pool(name="small", bufs=12))
         ps_t = ctx.enter_context(tc.psum_pool(name="ps_t", bufs=2))
         ps_s = ctx.enter_context(tc.psum_pool(name="ps_s", bufs=2))
@@ -47,9 +47,8 @@ def tile_palaceattention_t_kernel(tc, x, inter_palace_weight, out):
             xb = xpool.tile([P, NT, HD], BF16, name="xq%d" % b)
             src = x[b].rearrange("(p t) h -> p t h", t=NT)
             if b == 0:
-                for c in range(NT):
-                    cols = slice(c * (HD // NT), (c + 1) * (HD // NT))
-                    nc.sync.dma_start(out=xb[:, :, cols], in_=src[:, :, cols])
+                for t in range(NT):
+                    nc.sync.dma_start(out=xb[:, t, :], in_=src[:, t, :])
             else:
                 nc.sync.dma_start(out=xb[:], in_=src)
             xq.append(xb)
@@ -58,34 +57,22 @@ def tile_palaceattention_t_kernel(tc, x, inter_palace_weight, out):
 
         ident_f = const.tile([P, P], F32)
         make_identity(nc, ident_f[:])
-        en = const.tile([P, 1], F32)
-        nc.scalar.activation(out=en[:], in_=w_bf[:], func=ACT.Exp, scale=-1.0)
-        den = const.tile([P, 1], F32)
-        nc.vector.tensor_scalar_add(out=den[:], in0=en[:], scalar1=1.0)
-        sig = const.tile([P, 1], F32)
-        nc.vector.reciprocal(out=sig[:], in_=den[:])
-        sigp = const.tile([P, 1], F32)
-        nc.vector.tensor_scalar_mul(out=sigp[:], in0=sig[:], scalar1=SCALE)
-        diff = const.tile([P, 1], F32)
-        nc.vector.tensor_scalar(out=diff[:], in0=sigp[:], scalar1=-1.0, scalar2=SCALE,
-                                op0=ALU.mult, op1=ALU.add)
         par = const.tile([P, 2], F32)
         nc.vector.tensor_reduce(out=par[:], in_=ident_f[:].rearrange("p (c e) -> p e c", e=2),
                                 axis=AX.X, op=ALU.add)
-        sv = const.tile([P, 2], F32)
-        nc.vector.tensor_scalar(out=sv[:], in0=par[:], scalar1=diff[:, 0:1], scalar2=sigp[:, 0:1],
-                                op0=ALU.mult, op1=ALU.add)
-        mk = const.tile([P, NT, T], F32)
-        for it in range(NT):
-            if it > 0:
-                nc.vector.memset(mk[:, it, 0:it * P], 1.0)
-            nc.vector.tensor_copy(
-                out=mk[:, it, it * P:(it + 1) * P].rearrange("p (c e) -> p c e", e=2),
-                in_=sv[:].unsqueeze(1).to_broadcast([P, P // 2, 2]),
-            )
-            if it < NT - 1:
-                nc.vector.tensor_copy(out=mk[:, it, (it + 1) * P:T],
-                                      in_=sigp[:, 0:1].to_broadcast([P, T - (it + 1) * P]))
+        mk = const.tile([P, (2 * NT - 1) * P], F32)
+        nc.vector.memset(mk[:, 0:(NT - 1) * P], 1.0)
+        en = const.tile([P, 1], F32)
+        nc.scalar.activation(out=en[:], in_=w_bf[:], func=ACT.Exp, scale=-1.0)
+        den = const.tile([P, 1], F32)
+        nc.vector.tensor_scalar(out=den[:], in0=en[:], scalar1=1.0, scalar2=1.0 / SCALE, op0=ALU.add, op1=ALU.mult)
+        sigp = const.tile([P, 1], F32)
+        nc.vector.reciprocal(out=sigp[:], in_=den[:])
+        nc.vector.tensor_scalar(
+            out=mk[:, (NT - 1) * P:NT * P].rearrange("p (c e) -> p c e", e=2),
+            in0=par[:].unsqueeze(1).to_broadcast([P, P // 2, 2]),
+            scalar1=SCALE, scalar2=sigp[:, 0:1], op0=ALU.mult, op1=ALU.max)
+        nc.vector.tensor_copy(out=mk[:, NT * P:], in_=sigp[:, 0:1].to_broadcast([P, (NT - 1) * P]))
 
         qt, gq, qc, qs, tp_t = {}, {}, {}, {}, {}
         sps_t, s_t, negm_t, rs_t, e_t, rinv_t = {}, {}, {}, {}, {}, {}
@@ -150,7 +137,7 @@ def tile_palaceattention_t_kernel(tc, x, inter_palace_weight, out):
 
         def mask(g):
             s = sp.tile([P, T], F32, name="s")
-            nc.vector.tensor_tensor(out=s[:], in0=sps_t[g][:], in1=mk[:, g % NT, :], op=ALU.mult)
+            nc.vector.tensor_tensor(out=s[:], in0=sps_t[g][:], in1=mk[:, (NT - 1 - g % NT) * P:(2 * NT - 1 - g % NT) * P], op=ALU.mult)
             s_t[g] = s
 
         def rowmax(g):
@@ -226,54 +213,82 @@ def tile_palaceattention_t_kernel(tc, x, inter_palace_weight, out):
                 for op in mms[i:i + 1] + trs[i:i + 1]:
                     op()
 
-        def ok(i):
-            return 0 <= i < G
+        pairs = [(0, 0), (0, 1)]
+        for b in range(B - 1):
+            pairs += [(b, 2), (b + 1, 0), (b, 3), (b + 1, 1)]
+        pairs += [(B - 1, 2), (B - 1, 3)]
+        seq = [b * NT + it for b, it in pairs]
 
-        for c in range(NT):
-            weave([], tq_ops(0, c))
-            qt_exit(0, c)
-            if c == 0:
-                regroup(0)
-                mm = mm_ops(0)
+        def at(i):
+            return seq[i] if 0 <= i < G else None
+
+        qt_first = qtp.tile([P, NT, T], F32, name="qt")
+        qt[0] = qt_first
+        xf_first = xq[0][:].bitcast(F32)
+        s_first = ps_s.tile([P, T], F32, name="s_ps")
+        sps_t[0] = s_first
+        qv_first = qt_first[:].bitcast(BF16).rearrange("p c (k e) -> p c k e", e=2)
+
+        def mm_first(t):
+            for k in range(8):
+                nc.tensor.matmul(s_first[:, t * P:(t + 1) * P], lhsT=qv_first[:, k // 2, 0:P, k % 2],
+                                 rhs=qv_first[:, k // 2, t * P:(t + 1) * P, k % 2], start=(k == 0), stop=(k == 7))
+
+        for t in range(NT):
+            pool, tag = ((ps_t, "tp"), (ps_o, "o_ps"))[t % 2]
+            tp = pool.tile([P, NT, P], F32, name=tag)
+            for c in range(NT):
+                nc.tensor.transpose(tp[:, c, :], xf_first[:, t, c * P:(c + 1) * P], ident_f[:])
+            if t % 2 == 0:
+                nc.scalar.copy(out=qt_first[:, :, t * P:(t + 1) * P], in_=tp[:])
             else:
-                weave(mm[2 * c - 2:2 * c], [])
-        weave(mm[6:8], tq_ops(1, 0))
+                nc.vector.tensor_copy(out=qt_first[:, :, t * P:(t + 1) * P], in_=tp[:])
+            if t == 2:
+                mm_first(0)
+        regroup(0)
+        for t in range(1, NT):
+            mm_first(t)
+        for op in tq_ops(1, 0):
+            op()
         late = [4]
 
-        for g in range(1, G + 9):
-            ms = {1: [5, 6], 2: [7]}.get(g, [g + 5])
+        for g in range(1, G + 8):
+            ms = {1: [5, 6], 2: [7, 8]}.get(g, [g + 6])
             ms = [m for m in ms if m < G]
-            if ok(g - 3):
-                rowmax(g - 3)
-            if ok(g - 2):
-                mask(g - 2)
-            if ok(g - 7):
-                quant_e(g - 7)
-            if ok(g - 1):
+            g_mm, g_ts, g_mask, g_max, g_exp = at(g), at(g - 1), at(g - 2), at(g - 3), at(g - 3)
+            g_rc, g_te, g_ee, g_qe, g_mx = at(g - 5), at(g - 4), at(g - 4), at(g - 6), at(g - 6)
+            g_os, g_ov = at(g - 6), at(g - 7)
+            if g_max is not None:
+                rowmax(g_max)
+            if g_mask is not None:
+                mask(g_mask)
+            if g_qe is not None:
+                quant_e(g_qe)
+            if 0 <= g - 1 < G:
                 quant_q(g - 1)
-            if ok(g):
-                regroup(g)
-            if ok(g - 5):
-                recip(g - 5)
-            if ok(g - 8):
-                o_half(g - 8, 1, True)
-                store(g - 8)
+            if 0 <= g - 1 + 1 < G and g > 0:
+                regroup(g - 1 + 1)
+            if g_rc is not None:
+                recip(g_rc)
+            if g_ov is not None:
+                o_half(g_ov, 1, True)
+                store(g_ov)
             for m in late:
                 qt_exit(m // NT, m % NT)
-            if ok(g - 3):
-                expo(g - 3)
-            mm = mm_ops(g) if ok(g) else []
-            ts = ts_ops(g - 1) if ok(g - 1) else []
-            te = te_ops(g - 5) if ok(g - 5) else []
+            if g_exp is not None:
+                expo(g_exp)
+            mm = mm_ops(g_mm) if g_mm is not None else []
+            ts = ts_ops(g_ts) if g_ts is not None else []
+            te = te_ops(g_te) if g_te is not None else []
             tq = []
             for m in ms:
                 tq += tq_ops(m // NT, m % NT)
-            weave(mm[0:3], ts)
-            if ok(g - 7):
-                mx(g - 7)
-            weave(mm[3:8], te + tq)
-            if ok(g - 7):
-                o_half(g - 7, 0, False)
-            if ok(g - 5):
-                e_exit(g - 5)
+            weave(mm[0:2], ts)
+            if g_mx is not None:
+                mx(g_mx)
+            weave(mm[2:8], te + tq)
+            if g_os is not None:
+                o_half(g_os, 0, False)
+            if g_ee is not None:
+                e_exit(g_ee)
             late = ms

@@ -55,6 +55,8 @@ def tile_palaceattention_t_kernel(tc, x, inter_palace_weight, out):
         w_bf = const.tile([P, 1], BF16)
         nc.scalar.dma_start(out=w_bf[:], in_=inter_palace_weight.partition_broadcast(P))
 
+        zero = const.tile([P, T], BF16)
+        nc.vector.memset(zero[:], 0.0)
         ident_f = const.tile([P, P], F32)
         make_identity(nc, ident_f[:])
         par = const.tile([P, 2], F32)
@@ -222,6 +224,13 @@ def tile_palaceattention_t_kernel(tc, x, inter_palace_weight, out):
         def at(i):
             return seq[i] if 0 <= i < G else None
 
+        spare = ps_o.tile([P, T], F32, name="o_ps")
+
+        def warm(n):
+            nc.tensor.matmul(spare[:, 0:n], lhsT=zero[:, 0:P], rhs=zero[:, 0:n], start=True, stop=True)
+
+        for i in range(5):
+            warm(T)
         qt_first = qtp.tile([P, NT, T], F32, name="qt")
         qt[0] = qt_first
         xf_first = xq[0][:].bitcast(F32)
@@ -243,7 +252,10 @@ def tile_palaceattention_t_kernel(tc, x, inter_palace_weight, out):
                 nc.scalar.copy(out=qt_first[:, :, t * P:(t + 1) * P], in_=tp[:])
             else:
                 nc.vector.tensor_copy(out=qt_first[:, :, t * P:(t + 1) * P], in_=tp[:])
+            if t < 2:
+                warm(2 * P)
             if t == 2:
+                warm(P)
                 mm_first(0)
         regroup(0)
         for t in range(1, NT):

@@ -19,6 +19,13 @@ G = B * NT
 SCALE = HD ** -0.5
 FLOPS = 2 * B * T * T * HD * 2
 PIN = True
+LO, PAD = 8, 8
+SPLIT = (
+    ((P, T), (0, P), LO - 1),
+    ((2 * P, T), (0, 2 * P), LO - 1),
+    ((0, 2 * P), (2 * P, T), LO + T),
+    ((0, 3 * P), (3 * P, T), LO + T),
+)
 
 
 def tile_palaceattention_t_kernel(tc, x, inter_palace_weight, out):
@@ -77,6 +84,7 @@ def tile_palaceattention_t_kernel(tc, x, inter_palace_weight, out):
         nc.vector.tensor_copy(out=mk[:, NT * P:], in_=sigp[:, 0:1].to_broadcast([P, (NT - 1) * P]))
 
         qt, gq, qc, qs, tp_t = {}, {}, {}, {}, {}
+        row_t = {}
         sps_t, s_t, negm_t, rs_t, e_t, rinv_t = {}, {}, {}, {}, {}, {}
         tpe_t, ge_t, ec_t, es_t, ops_t, osb_t = {}, {}, {}, {}, {}, {}
         QW = HD // NT
@@ -138,20 +146,30 @@ def tile_palaceattention_t_kernel(tc, x, inter_palace_weight, out):
             ]
 
         def mask(g):
-            s = sp.tile([P, T], F32, name="s")
-            nc.vector.tensor_tensor(out=s[:], in0=sps_t[g][:], in1=mk[:, (NT - 1 - g % NT) * P:(2 * NT - 1 - g % NT) * P], op=ALU.mult)
-            s_t[g] = s
+            it = g % NT
+            row = sp.tile([P, LO + T + PAD], F32, name="row")
+            s = row[:, LO:LO + T]
+            s_t[g], row_t[g] = s, row
+            plain, masked, peak = SPLIT[it]
+            nc.vector.tensor_scalar(out=s[:, plain[0]:plain[1]], in0=sps_t[g][:, plain[0]:plain[1]],
+                                    scalar1=(sigp[:, 0:1] if it < 2 else 1.0), scalar2=None, op0=ALU.mult,
+                                    op1=ALU.max, accum_out=row[:, peak:peak + 1])
+            k0 = (NT - 1 - it) * P
+            nc.vector.tensor_tensor(out=s[:, masked[0]:masked[1]], in0=sps_t[g][:, masked[0]:masked[1]],
+                                    in1=mk[:, k0 + masked[0]:k0 + masked[1]], op=ALU.mult)
 
         def rowmax(g):
             negm = small.tile([P, 1], F32, name="negm")
-            nc.vector.tensor_reduce(out=negm[:], in_=s_t[g][:], axis=AX.X, op=ALU.max, negate=True)
+            masked, peak = SPLIT[g % NT][1:]
+            span = row_t[g][:, peak:LO + masked[1]] if peak < LO else row_t[g][:, LO + masked[0]:peak + 1]
+            nc.vector.tensor_reduce(out=negm[:], in_=span, axis=AX.X, op=ALU.max, negate=True)
             negm_t[g] = negm
 
         def expo(g):
             e = ep.tile([P, T], BF16, name="e")
             rs = small.tile([P, 1], F32, name="rs")
             nc.scalar.activation(out=e[:].rearrange("p (u k j) -> p u k j", u=2, j=2),
-                                 in_=s_t[g][:].rearrange("p (u j k) -> p u k j", u=2, j=2),
+                                 in_=s_t[g].rearrange("p (u j k) -> p u k j", u=2, j=2),
                                  func=ACT.Exp, bias=negm_t[g][:, 0:1], scale=1.0, accum_out=rs[:, 0:1])
             e_t[g], rs_t[g] = e, rs
 

@@ -285,11 +285,9 @@ def tile_palaceattention_t_kernel(tc, x, inter_palace_weight, out):
         for g in range(1, G + 8):
             ms = {1: [5, 6], 2: [7, 8]}.get(g, [g + 6])
             ms = [m for m in ms if m < G]
-            g_mm, g_ts, g_mask, g_max, g_exp = at(g), at(g - 1), at(g - 2), at(g - 3), at(g - 3)
+            g_mm, g_ts, g_mask, g_max, g_exp = at(g), at(g - 1), at(g - 2), at(g - 2), at(g - 3)
             g_rc, g_te, g_ee, g_qe, g_mx = at(g - 5), at(g - 4), at(g - 4), at(g - 6), at(g - 6)
             g_os, g_ov = at(g - 6), at(g - 7)
-            if g_max is not None:
-                rowmax(g_max)
             if g_mask is not None:
                 mask(g_mask)
             if g_qe is not None:
@@ -298,11 +296,13 @@ def tile_palaceattention_t_kernel(tc, x, inter_palace_weight, out):
                 quant_q(g - 1)
             if 0 <= g - 1 + 1 < G and g > 0:
                 regroup(g - 1 + 1)
-            if g_rc is not None:
-                recip(g_rc)
             if g_ov is not None:
                 o_half(g_ov, 1, True)
                 store(g_ov)
+            if g_max is not None:
+                rowmax(g_max)
+            if g_rc is not None:
+                recip(g_rc)
             for m in late:
                 qt_exit(m // NT, m % NT)
             if g_exp is not None:
@@ -313,7 +313,8 @@ def tile_palaceattention_t_kernel(tc, x, inter_palace_weight, out):
             tq = []
             for m in ms:
                 tq += tq_ops(m // NT, m % NT)
-            weave(mm[0:2], ts)
+            weave(mm[0:1], ts)
+            weave(mm[1:2], [])
             if g_mx is not None:
                 mx(g_mx)
             weave(mm[2:8], te + tq)

@@ -224,9 +224,9 @@ def tile_palaceattention_t_kernel(tc, x, inter_palace_weight, out):
                 nc.scalar.activation(out=osb_t[g][:, cols], in_=ops_t[g][hh][:], func=ACT.Copy,
                                      scale=rinv_t[g][:, 0:1])
 
-        def store(g):
+        def store(g, c0=0, c1=HD):
             b, it = divmod(g, NT)
-            nc.sync.dma_start(out=out[b].rearrange("(p t) h -> p t h", t=NT)[:, it, :], in_=osb_t[g][:])
+            nc.sync.dma_start(out=out[b].rearrange("(p t) h -> p t h", t=NT)[:, it, c0:c1], in_=osb_t[g][:, c0:c1])
 
         def weave(mms, trs):
             for i in range(max(len(mms), len(trs))):
@@ -238,6 +238,8 @@ def tile_palaceattention_t_kernel(tc, x, inter_palace_weight, out):
             pairs += [(b, 2), (b + 1, 0), (b, 3), (b + 1, 1)]
         pairs += [(B - 1, 2), (B - 1, 3)]
         seq = [b * NT + it for b, it in pairs]
+
+        halves = seq[28:]
 
         def at(i):
             return seq[i] if 0 <= i < G else None
@@ -282,12 +284,12 @@ def tile_palaceattention_t_kernel(tc, x, inter_palace_weight, out):
             op()
         late = [4]
 
-        for g in range(1, G + 8):
+        for g in range(1, G + 7):
             ms = {1: [5, 6], 2: [7, 8]}.get(g, [g + 6])
             ms = [m for m in ms if m < G]
             g_mm, g_ts, g_mask, g_max, g_exp = at(g), at(g - 1), at(g - 2), at(g - 2), at(g - 3)
-            g_rc, g_te, g_ee, g_qe, g_mx = at(g - 5), at(g - 4), at(g - 4), at(g - 6), at(g - 6)
-            g_os, g_ov = at(g - 6), at(g - 7)
+            g_rc, g_te, g_ee, g_qe, g_mx = at(g - 4), at(g - 3), at(g - 3), at(g - 5), at(g - 5)
+            g_os, g_ov = at(g - 5), at(g - 6)
             if g_mask is not None:
                 mask(g_mask)
             if g_qe is not None:
@@ -298,15 +300,15 @@ def tile_palaceattention_t_kernel(tc, x, inter_palace_weight, out):
                 regroup(g - 1 + 1)
             if g_ov is not None:
                 o_half(g_ov, 1, True)
-                store(g_ov)
+                store(g_ov, T if g_ov in halves else 0)
             if g_max is not None:
                 rowmax(g_max)
             if g_rc is not None:
                 recip(g_rc)
-            for m in late:
-                qt_exit(m // NT, m % NT)
             if g_exp is not None:
                 expo(g_exp)
+            for m in late:
+                qt_exit(m // NT, m % NT)
             mm = mm_ops(g_mm) if g_mm is not None else []
             ts = ts_ops(g_ts) if g_ts is not None else []
             te = te_ops(g_te) if g_te is not None else []
@@ -320,6 +322,8 @@ def tile_palaceattention_t_kernel(tc, x, inter_palace_weight, out):
             weave(mm[2:8], te + tq)
             if g_os is not None:
                 o_half(g_os, 0, False)
+                if g_os in halves:
+                    store(g_os, 0, T)
             if g_ee is not None:
                 e_exit(g_ee)
             late = ms

from contextlib import ExitStack

import concourse.mybir as mybir
from concourse.masks import make_identity

F32 = mybir.dt.float32
BF16 = mybir.dt.bfloat16
U32 = mybir.dt.uint32
U8 = mybir.dt.uint8
FP8X4 = mybir.dt.float8_e4m3fn_x4
ALU = mybir.AluOpType
ACT = mybir.ActivationFunctionType
AX = mybir.AxisListType

B, T, HD = 8, 512, 1024
P = 128
NT = T // P
G = B * NT
SCALE = HD ** -0.5
FLOPS = 2 * B * T * T * HD * 2
PIN = True
LO, PAD = 8, 8
SPLIT = (
    ((P, T), (0, P), LO - 1),
    ((2 * P, T), (0, 2 * P), LO - 1),
    ((0, 2 * P), (2 * P, T), LO + T),
    ((0, 3 * P), (3 * P, T), LO + T),
)


def tile_palaceattention_t_kernel(tc, x, inter_palace_weight, out):
    nc = tc.nc
    with ExitStack() as ctx:
        const = ctx.enter_context(tc.tile_pool(name="const", bufs=1))
        xpool = ctx.enter_context(tc.tile_pool(name="xpool", bufs=1))
        qtp = ctx.enter_context(tc.tile_pool(name="qtp", bufs=3))
        gqp = ctx.enter_context(tc.tile_pool(name="gqp", bufs=1))
        qcp = ctx.enter_context(tc.tile_pool(name="qcp", bufs=3))
        sp = ctx.enter_context(tc.tile_pool(name="sp", bufs=8))
        ep = ctx.enter_context(tc.tile_pool(name="ep", bufs=3))
        gep = ctx.enter_context(tc.tile_pool(name="gep", bufs=3))
        ecp = ctx.enter_context(tc.tile_pool(name="ecp", bufs=3))
        opool = ctx.enter_context(tc.tile_pool(name="opool", bufs=8))
        small = ctx.enter_context(tc.tile_pool(name="small", bufs=12))
        ps_t = ctx.enter_context(tc.psum_pool(name="ps_t", bufs=2))
        ps_s = ctx.enter_context(tc.psum_pool(name="ps_s", bufs=2))
        ps_e = ctx.enter_context(tc.psum_pool(name="ps_e", bufs=1))
        ps_o = ctx.enter_context(tc.psum_pool(name="ps_o", bufs=3))
        if PIN:
            ctx.enter_context(tc.manual_schedule())

        xq = []
        for b in range(B):
            xb = xpool.tile([P, NT, HD], BF16, name="xq%d" % b)
            src = x[b].rearrange("(p t) h -> p t h", t=NT)
            if b == 0:
                for t in range(NT):
                    nc.sync.dma_start(out=xb[:, t, :], in_=src[:, t, :])
            else:
                nc.sync.dma_start(out=xb[:], in_=src)
            xq.append(xb)
        w_bf = const.tile([P, 1], BF16)
        nc.scalar.dma_start(out=w_bf[:], in_=inter_palace_weight.partition_broadcast(P))

        zero = const.tile([P, T], BF16)
        nc.vector.memset(zero[:], 0.0)
        ident_f = const.tile([P, P], F32)
        make_identity(nc, ident_f[:])
        par = const.tile([P, 2], F32)
        nc.vector.tensor_reduce(out=par[:], in_=ident_f[:].rearrange("p (c e) -> p e c", e=2),
                                axis=AX.X, op=ALU.add)
        mk = const.tile([P, (2 * NT - 1) * P], F32)
        nc.vector.memset(mk[:, 0:(NT - 1) * P], 1.0)
        en = const.tile([P, 1], F32)
        nc.scalar.activation(out=en[:], in_=w_bf[:], func=ACT.Exp, scale=-1.0)
        den = const.tile([P, 1], F32)
        nc.vector.tensor_scalar(out=den[:], in0=en[:], scalar1=1.0, scalar2=1.0 / SCALE, op0=ALU.add, op1=ALU.mult)
        sigp = const.tile([P, 1], F32)
        nc.vector.reciprocal(out=sigp[:], in_=den[:])
        nc.vector.tensor_scalar(
            out=mk[:, (NT - 1) * P:NT * P].rearrange("p (c e) -> p c e", e=2),
            in0=par[:].unsqueeze(1).to_broadcast([P, P // 2, 2]),
            scalar1=SCALE, scalar2=sigp[:, 0:1], op0=ALU.mult, op1=ALU.max)
        nc.vector.tensor_copy(out=mk[:, NT * P:], in_=sigp[:, 0:1].to_broadcast([P, (NT - 1) * P]))

        qt, gq, qc, qs, tp_t = {}, {}, {}, {}, {}
        row_t = {}
        sps_t, s_t, negm_t, rs_t, e_t, rinv_t = {}, {}, {}, {}, {}, {}
        tpe_t, ge_t, ec_t, es_t, ops_t, osb_t = {}, {}, {}, {}, {}, {}
        QW = HD // NT

        def tq_ops(b, c):
            if c == 0:
                qt_new = qtp.tile([P, NT, T], F32, name="qt")
                qt[b] = qt_new
            xf = xq[b][:].bitcast(F32)
            tp = ps_t.tile([P, NT, P], F32, name="tp")
            tp_t[(b, c)] = tp
            return [
                (lambda t=t: nc.tensor.transpose(tp[:, t, :], xf[:, t, c * P:(c + 1) * P], ident_f[:]))
                for t in range(NT)
            ]

        def qt_exit(b, c):
            nc.scalar.copy(out=qt[b][:, c, :], in_=tp_t[(b, c)][:].rearrange("p t k -> p (t k)"))

        def regroup(n):
            b, c = divmod(n, NT)
            h0 = c * QW
            gq_new = gqp.tile([P, QW, NT], BF16, name="gq", align_bytes=64)
            gq[n] = gq_new
            nc.gpsimd.tensor_scalar(out=gq_new[:], in0=xq[b][:, :, h0:h0 + QW].rearrange("p t h -> p h t"),
                                    scalar1=1.0, scalar2=0.0, op0=ALU.mult, op1=ALU.add)

        def quant_q(n):
            b, c = divmod(n, NT)
            if c == 0:
                qc_new = qcp.tile([P, HD], U32, name="qc", align_bytes=64)
                qs_new = qcp.tile([P, HD], U8, name="qs", align_bytes=64)
                qc[b], qs[b] = qc_new, qs_new
            h0 = c * QW
            nc.vector.quantize_mx(
                out=qc[b][:, h0:h0 + QW].bitcast(FP8X4),
                scales=qs[b][:, h0:h0 + QW],
                in_=gq[n][:].rearrange("p h t -> p (h t)"),
            )

        def mm_ops(g):
            b, it = divmod(g, NT)
            qv = qt[b][:].bitcast(BF16).rearrange("p c (k e) -> p c k e", e=2)
            s_ps = ps_s.tile([P, T], F32, name="s_ps")
            sps_t[g] = s_ps
            return [
                (lambda k=k: nc.tensor.matmul(
                    s_ps[:, it * P:T], lhsT=qv[:, k // 2, it * P:(it + 1) * P, k % 2],
                    rhs=qv[:, k // 2, it * P:T, k % 2], start=(k == 0), stop=(k == 7)))
                for k in range(8)
            ]

        def ts_ops(g):
            b, it = divmod(g, NT)
            return [
                (lambda jt=jt: nc.tensor.transpose(sps_t[g][:, jt * P:(jt + 1) * P],
                                                   s_t[b * NT + jt][:, it * P:(it + 1) * P], ident_f[:]))
                for jt in range(it)
            ]

        def mask(g):
            it = g % NT
            row = sp.tile([P, LO + T + PAD], F32, name="row")
            s = row[:, LO:LO + T]
            s_t[g], row_t[g] = s, row
            plain, masked, peak = SPLIT[it]
            nc.vector.tensor_scalar(out=s[:, plain[0]:plain[1]], in0=sps_t[g][:, plain[0]:plain[1]],
                                    scalar1=(sigp[:, 0:1] if it < 2 else 1.0), scalar2=None, op0=ALU.mult,
                                    op1=ALU.max, accum_out=row[:, peak:peak + 1])
            k0 = (NT - 1 - it) * P
            nc.vector.tensor_tensor(out=s[:, masked[0]:masked[1]], in0=sps_t[g][:, masked[0]:masked[1]],
                                    in1=mk[:, k0 + masked[0]:k0 + masked[1]], op=ALU.mult)

        def rowmax(g):
            negm = small.tile([P, 1], F32, name="negm")
            masked, peak = SPLIT[g % NT][1:]
            span = row_t[g][:, peak:LO + masked[1]] if peak < LO else row_t[g][:, LO + masked[0]:peak + 1]
            nc.vector.tensor_reduce(out=negm[:], in_=span, axis=AX.X, op=ALU.max, negate=True)
            negm_t[g] = negm

        def expo(g):
            e = ep.tile([P, T], BF16, name="e")
            rs = small.tile([P, 1], F32, name="rs")
            nc.scalar.activation(out=e[:].rearrange("p (u k j) -> p u k j", u=2, j=2),
                                 in_=s_t[g].rearrange("p (u j k) -> p u k j", u=2, j=2),
                                 func=ACT.Exp, bias=negm_t[g][:, 0:1], scale=1.0, accum_out=rs[:, 0:1])
            e_t[g], rs_t[g] = e, rs

        def recip(g):
            rinv = small.tile([P, 1], F32, name="rinv")
            nc.vector.reciprocal(out=rinv[:], in_=rs_t[g][:])
            rinv_t[g] = rinv

        def te_ops(g):
            ew = e_t[g][:].bitcast(F32)
            tpe = ps_e.tile([P, 2, P], F32, name="tpe")
            tpe_t[g] = tpe
            return [
                (lambda u=u: nc.tensor.transpose(tpe[:, u, :], ew[:, u * P:(u + 1) * P], ident_f[:]))
                for u in range(2)
            ]

        def e_exit(g):
            ge = gep.tile([P, P, NT], BF16, name="ge", align_bytes=64)
            nc.scalar.copy(out=ge[:].rearrange("q i t -> q (i t)").bitcast(F32).rearrange("q (i u) -> q i u", u=2),
                           in_=tpe_t[g][:].rearrange("q u i -> q i u"))
            ge_t[g] = ge

        def quant_e(g):
            ec = ecp.tile([P, P], U32, name="ec", align_bytes=64)
            es = ecp.tile([P, P], U8, name="es", align_bytes=64)
            nc.vector.quantize_mx(out=ec[:].bitcast(FP8X4), scales=es[:],
                                  in_=ge_t[g][:].rearrange("q i t -> q (i t)"))
            ec_t[g], es_t[g] = ec, es

        def mx(g):
            b = g // NT
            o_pss = []
            for hh in range(2):
                cols = slice(hh * 512, (hh + 1) * 512)
                o_ps = ps_o.tile([P, 512], F32, name="o_ps")
                nc.tensor.matmul_mx(out=o_ps[:], lhsT=ec_t[g][:].bitcast(FP8X4), lhsT_scale=es_t[g][:],
                                    rhs=qc[b][:, cols].bitcast(FP8X4), rhs_scale=qs[b][:, cols],
                                    start=True, stop=True)
                o_pss.append(o_ps)
            ops_t[g] = o_pss

        def o_half(g, hh, on_vector):
            if g not in osb_t:
                o_new = opool.tile([P, HD], F32, name="o_sb")
                osb_t[g] = o_new
            cols = slice(hh * 512, (hh + 1) * 512)
            if on_vector:
                nc.vector.tensor_scalar_mul(out=osb_t[g][:, cols], in0=ops_t[g][hh][:],
                                            scalar1=rinv_t[g][:, 0:1])
            else:
                nc.scalar.activation(out=osb_t[g][:, cols], in_=ops_t[g][hh][:], func=ACT.Copy,
                                     scale=rinv_t[g][:, 0:1])

        def store(g, c0=0, c1=HD):
            b, it = divmod(g, NT)
            nc.sync.dma_start(out=out[b].rearrange("(p t) h -> p t h", t=NT)[:, it, c0:c1], in_=osb_t[g][:, c0:c1])

        def weave(mms, trs):
            for i in range(max(len(mms), len(trs))):
                for op in mms[i:i + 1] + trs[i:i + 1]:
                    op()

        pairs = [(0, 0), (0, 1)]
        for b in range(B - 1):
            pairs += [(b, 2), (b + 1, 0), (b, 3), (b + 1, 1)]
        pairs += [(B - 1, 2), (B - 1, 3)]
        seq = [b * NT + it for b, it in pairs]

        halves = seq[28:]

        def at(i):
            return seq[i] if 0 <= i < G else None

        spare = ps_o.tile([P, T], F32, name="o_ps")

        def warm(n):
            nc.tensor.matmul(spare[:, 0:n], lhsT=zero[:, 0:P], rhs=zero[:, 0:n], start=True, stop=True)

        for i in range(5):
            warm(T)
        qt_first = qtp.tile([P, NT, T], F32, name="qt")
        qt[0] = qt_first
        xf_first = xq[0][:].bitcast(F32)
        s_first = ps_s.tile([P, T], F32, name="s_ps")
        sps_t[0] = s_first
        qv_first = qt_first[:].bitcast(BF16).rearrange("p c (k e) -> p c k e", e=2)

        def mm_first(t):
            for k in range(8):
                nc.tensor.matmul(s_first[:, t * P:(t + 1) * P], lhsT=qv_first[:, k // 2, 0:P, k % 2],
                                 rhs=qv_first[:, k // 2, t * P:(t + 1) * P, k % 2], start=(k == 0), stop=(k == 7))

        for t in range(NT):
            pool, tag = ((ps_t, "tp"), (ps_o, "o_ps"))[t % 2]
            tp = pool.tile([P, NT, P], F32, name=tag)
            for c in range(NT):
                nc.tensor.transpose(tp[:, c, :], xf_first[:, t, c * P:(c + 1) * P], ident_f[:])
            if t % 2 == 0:
                nc.scalar.copy(out=qt_first[:, :, t * P:(t + 1) * P], in_=tp[:])
            else:
                nc.vector.tensor_copy(out=qt_first[:, :, t * P:(t + 1) * P], in_=tp[:])
            if t < 2:
                warm(2 * P)
            if t == 2:
                warm(P)
                mm_first(0)
        regroup(0)
        for t in range(1, NT):
            mm_first(t)
        for op in tq_ops(1, 0):
            op()
        late = [4]

        for g in range(1, G + 7):
            ms = {1: [5, 6], 2: [7, 8]}.get(g, [g + 6])
            ms = [m for m in ms if m < G]
            g_mm, g_ts, g_mask, g_max, g_exp = at(g), at(g - 1), at(g - 2), at(g - 2), at(g - 3)
            g_rc, g_te, g_ee, g_qe, g_mx = at(g - 4), at(g - 3), at(g - 3), at(g - 5), at(g - 5)
            g_os, g_ov = at(g - 5), at(g - 6)
            if g_mask is not None:
                mask(g_mask)
            if g_qe is not None:
                quant_e(g_qe)
            if 0 <= g - 1 < G:
                quant_q(g - 1)
            if 0 <= g - 1 + 1 < G and g > 0:
                regroup(g - 1 + 1)
            if g_ov is not None:
                o_half(g_ov, 1, True)
                store(g_ov, T if g_ov in halves else 0)
            if g_max is not None:
                rowmax(g_max)
            if g_rc is not None:
                recip(g_rc)
            if g_exp is not None:
                expo(g_exp)
            for m in late:
                qt_exit(m // NT, m % NT)
            mm = mm_ops(g_mm) if g_mm is not None else []
            ts = ts_ops(g_ts) if g_ts is not None else []
            te = te_ops(g_te) if g_te is not None else []
            tq = []
            for m in ms:
                tq += tq_ops(m // NT, m % NT)
            weave(mm[0:1], ts)
            weave(mm[1:2], [])
            if g_mx is not None:
                mx(g_mx)
            weave(mm[2:8], te + tq)
            if g_os is not None:
                o_half(g_os, 0, False)
                if g_os in halves:
                    store(g_os, 0, T)
            if g_ee is not None:
                e_exit(g_ee)
            late = ms
